import numpy as np
import ml_dtypes


def mxq(x, axis, fmt="e4m3"):
    dtype, down = {"e4m3": (ml_dtypes.float8_e4m3fn, 7), "e5m2": (ml_dtypes.float8_e5m2, 14)}[fmt]
    v = np.moveaxis(np.asarray(x, np.float32).astype(ml_dtypes.bfloat16).astype(np.float64), axis, -1)
    blocks = v.reshape(v.shape[:-1] + (-1, 32))
    amax = np.abs(blocks).max(-1, keepdims=True)
    byte = np.maximum(np.where(amax > 0, np.frexp(amax)[1] - 1 + 127, 0) - down, 1)
    scale = np.exp2(byte - 127.0)
    codes = (blocks / scale).astype(np.float32).astype(dtype).astype(np.float64)
    return np.moveaxis((codes * scale).reshape(v.shape), -1, axis)


WIDE = False


def mx_kscale(k):
    if not WIDE:
        return np.ones(k)
    levels = np.array([20, -20, 10, -10, 0])
    a = np.random.permutation(np.resize(levels, k // 512 * 4)).reshape(k // 512, 4)
    idx = np.arange(k)
    return np.exp2(a[idx // 512, idx % 128 // 32])


BF16 = ml_dtypes.bfloat16


def bf(x):
    return np.asarray(x, np.float32).astype(BF16)


def f64(x):
    return np.asarray(x).astype(np.float64)


N, M0, D0, M1, D1, M2, D2 = 1024, 512, 1, 512, 3, 256, 5
IRREPS = [(M0, D0), (M1, D1), (M2, D2)]
IN_DIM = sum(m * d for m, d in IRREPS)


def setup_inputs():
    s0, s1 = mx_kscale(M0), mx_kscale(M1)
    sg = np.concatenate([np.repeat(s0, D0), np.repeat(s1, D1), np.ones(M2 * D2)])
    x = np.random.standard_normal((N, IN_DIM))
    w0 = np.random.standard_normal((M0, M0)) * 0.4 / s0[None, :]
    w1 = np.random.standard_normal((M1, M1)) * 0.4 / s1[None, :]
    w2 = np.random.standard_normal((M2, M2)) * 0.4
    g = np.random.standard_normal((N, IN_DIM)) * np.exp2(np.random.randint(-12, 1, (N, 1))) * 8.0 * sg
    return {"x": bf(x), "w0": bf(w0), "w1": bf(w1), "w2": bf(w2), "grad_out": bf(g)}


def reference(x, w0, w1, w2, grad_out):
    g = f64(grad_out)
    outs = []
    off = 0
    for (mul, d), w, quantised in zip(IRREPS, [f64(w0), f64(w1), f64(w2)], [True, True, False]):
        blk = g[:, off:off + mul * d].reshape(N, mul, d)
        if quantised:
            y = mxq(blk, 1, "e5m2").transpose(0, 2, 1) @ mxq(w, 1, "e4m3").T
        else:
            y = blk.transpose(0, 2, 1) @ w.T
        y = (1.0 / np.sqrt(mul)) * y.transpose(0, 2, 1)
        outs.append(y.reshape(N, mul * d))
        off += mul * d
    return np.concatenate(outs, axis=-1)

@@ -1,0 +1,217 @@
+import math
+from contextlib import ExitStack
+
+import concourse.mybir as mybir
+from concourse.masks import make_identity
+
+F32 = mybir.dt.float32
+BF16 = mybir.dt.bfloat16
+U32 = mybir.dt.uint32
+U8 = mybir.dt.uint8
+E4X4 = mybir.dt.float8_e4m3fn_x4
+E5X4 = mybir.dt.float8_e5m2_x4
+COPY = mybir.ActivationFunctionType.Copy
+MULT = mybir.AluOpType.mult
+ADD = mybir.AluOpType.add
+
+P = 128
+TOKENS = 1024
+NT = TOKENS // P
+M01 = 512
+M2 = 256
+D1 = 3
+D2 = 5
+OFF1 = M01
+OFF2 = M01 + M01 * D1
+COLS = OFF2 + M2 * D2
+S01 = 1.0 / math.sqrt(M01)
+S2 = 1.0 / math.sqrt(M2)
+CHUNKS = ((0, 102), (102, 102), (204, 52))
+
+FLOPS = 2 * TOKENS * (M01 * M01 * (1 + D1) + M2 * M2 * D2)
+BYTES = 2 * (TOKENS * COLS + 2 * M01 * M01 + M2 * M2) + 4 * TOKENS * COLS
+
+MANUAL = False
+
+
+def tile_linear_kernel(tc, x, w0, w1, w2, grad_out, out):
+    nc = tc.nc
+    with ExitStack() as ctx:
+        keep = ctx.enter_context(tc.tile_pool(name="keep", bufs=1))
+        work = ctx.enter_context(tc.tile_pool(name="work", bufs=2))
+        outs = ctx.enter_context(tc.tile_pool(name="outs", bufs=3))
+        psum = ctx.enter_context(tc.psum_pool(name="psum", bufs=8))
+        if MANUAL:
+            ctx.enter_context(tc.manual_schedule())
+
+        g_sb = [keep.tile([P, COLS], BF16, name="g%d" % k) for k in range(NT)]
+        w_raw = [keep.tile([P, 4 * M01], BF16, name="wraw%d" % b) for b in range(2)]
+        w2_raw = keep.tile([P, 2 * M2], BF16, name="w2raw")
+
+        def load_g(k):
+            nc.sync.dma_start(out=g_sb[k][:], in_=grad_out[k * P:(k + 1) * P, :])
+
+        load_g(0)
+        for b, w in enumerate((w0, w1)):
+            nc.sync.dma_start(
+                out=w_raw[b][:].rearrange("p (a w) -> p a w", a=4),
+                in_=w.rearrange("(a p) w -> p a w", p=P),
+            )
+        nc.sync.dma_start(
+            out=w2_raw[:].rearrange("p (a w) -> p a w", a=2),
+            in_=w2.rearrange("(a p) w -> p a w", p=P),
+        )
+        for k in range(1, NT):
+            load_g(k)
+
+        ident = keep.tile([P, P], F32, name="ident")
+        make_identity(nc, ident[:])
+
+        def bank(name):
+            return psum.tile([P, 512], F32, name=name, tag="bank")
+
+        def presort(k):
+            srt = work.tile([P, M01 * D1], BF16, name="srt", tag="srt", bufs=3)
+            nc.gpsimd.tensor_scalar(
+                out=srt[:].rearrange("p (i w) -> p i w", i=D1),
+                in0=g_sb[k][:, OFF1:OFF2].rearrange("p (w i) -> p i w", i=D1),
+                scalar1=1.0, scalar2=0.0, op0=MULT, op1=ADD,
+            )
+            return srt
+
+        def word_transposes(rows):
+            banks = []
+            for b in range(2):
+                t = bank("tw")
+                for r in range(2):
+                    for h in range(2):
+                        nc.tensor.transpose(
+                            out=t[:, (2 * r + h) * P:(2 * r + h + 1) * P],
+                            in_=rows[2 * b + r][:, h * P:(h + 1) * P],
+                            identity=ident[:],
+                        )
+                banks.append(t)
+            return banks
+
+        def regroup(banks, grouped, engines):
+            g32 = grouped[:].bitcast(F32).rearrange("p (r n h) -> p r n h", r=4, n=P, h=2)
+            for b in range(2):
+                src = banks[b][:].rearrange("p (r h n) -> p r n h", r=2, h=2, n=P)
+                dst = g32[:, 2 * b:2 * b + 2, :, :]
+                if engines[b] == "v":
+                    nc.vector.tensor_copy(out=dst, in_=src)
+                else:
+                    nc.scalar.copy(out=dst, in_=src)
+
+        w_codes = [keep.tile([P, M01], U32, name="wc%d" % b, align_bytes=64) for b in range(2)]
+        w_scales = [keep.tile([P, M01], U8, name="ws%d" % b, align_bytes=64) for b in range(2)]
+        w_grouped = [keep.tile([P, 4 * M01], BF16, name="wg%d" % b, align_bytes=64) for b in range(2)]
+        w2t = keep.tile([P, 2 * M2], BF16, name="w2t")
+
+        def t_block2(k):
+            g32 = g_sb[k][:].bitcast(F32)[:, OFF2 // 2:COLS // 2].rearrange("p (j s) -> p s j", s=D2)
+            ta = bank("tb")
+            for s in range(4):
+                nc.tensor.transpose(out=ta[:, s * P:(s + 1) * P], in_=g32[:, s, :], identity=ident[:])
+            tb = bank("tb")
+            nc.tensor.transpose(out=tb[:, 0:P], in_=g32[:, 4, :], identity=ident[:])
+            return ta, tb
+
+        def evac_block2(tabs):
+            gt2 = work.tile([P, D2 * P], F32, name="gt2", tag="gt2")
+            nc.vector.tensor_copy(out=gt2[:, 0:512], in_=tabs[0][:])
+            nc.vector.tensor_copy(out=gt2[:, 512:640], in_=tabs[1][:, 0:P])
+            return gt2
+
+        def t_block01(k, srt):
+            g32 = g_sb[k][:].bitcast(F32)
+            s32 = srt[:].bitcast(F32)
+            rows = [g32[:, 0:256]] + [s32[:, 256 * i:256 * (i + 1)] for i in range(D1)]
+            return word_transposes(rows)
+
+        def quantise_g(grouped):
+            codes = work.tile([P, 4 * P], U32, name="gc", tag="gc", align_bytes=64)
+            scales = work.tile([P, 4 * P], U8, name="gs", tag="gs", align_bytes=64)
+            nc.vector.quantize_mx(out=codes[:].bitcast(E5X4), scales=scales[:], in_=grouped[:])
+            return codes, scales
+
+        srts = {0: presort(0), 1: presort(1)}
+        tb_next = t_block2(0)
+        wbanks = []
+        for b in range(2):
+            w32 = w_raw[b][:].bitcast(F32)
+            wbanks.append(word_transposes([w32[:, 256 * a:256 * (a + 1)] for a in range(4)]))
+        gt2_next = evac_block2(tb_next)
+        for b in range(2):
+            regroup(wbanks[b], w_grouped[b], ("s", "v"))
+        tw2 = bank("tw2")
+        w232 = w2_raw[:].bitcast(F32)
+        for a in range(2):
+            nc.tensor.transpose(out=tw2[:, a * P:(a + 1) * P], in_=w232[:, a * P:(a + 1) * P], identity=ident[:])
+        ta_next = t_block01(0, srts[0])
+        for b in range(2):
+            nc.vector.quantize_mx(out=w_codes[b][:].bitcast(E4X4), scales=w_scales[b][:], in_=w_grouped[b][:])
+        nc.scalar.copy(
+            out=w2t[:].rearrange("p (e a u) -> p e a u", e=2, a=2, u=P),
+            in_=tw2[:, 0:2 * P].bitcast(BF16).rearrange("p (a u e) -> p e a u", a=2, u=P, e=2),
+        )
+        grouped = work.tile([P, 16 * P], BF16, name="grp", tag="grp", align_bytes=64)
+        regroup(ta_next, grouped, ("s", "v"))
+        q_next = quantise_g(grouped)
+
+        for k in range(NT):
+            codes, scales = q_next
+            gt2 = gt2_next
+            rows = slice(k * P, (k + 1) * P)
+            if k + 2 < NT:
+                srts[k + 2] = presort(k + 2)
+            if k + 1 < NT:
+                ta_next = t_block01(k + 1, srts[k + 1])
+                tb_next = t_block2(k + 1)
+            accs = []
+            for r in range(4):
+                acc = bank("acc")
+                b = min(r, 1)
+                nc.tensor.matmul_mx(
+                    out=acc[:],
+                    lhsT=codes[:, r * P:(r + 1) * P].bitcast(E5X4),
+                    lhsT_scale=scales[:, r * P:(r + 1) * P],
+                    rhs=w_codes[b][:].bitcast(E4X4),
+                    rhs_scale=w_scales[b][:],
+                    start=True, stop=True,
+                )
+                accs.append(acc)
+            if k + 1 < NT:
+                grouped = work.tile([P, 16 * P], BF16, name="grp", tag="grp", align_bytes=64)
+                regroup(ta_next, grouped, ("v", "v"))
+                gt2_next = evac_block2(tb_next)
+            o0 = outs.tile([P, M01], F32, name="o0", tag="o0")
+            nc.scalar.activation(out=o0[:], in_=accs[0][:], func=COPY, scale=S01)
+            nc.sync.dma_start(out=out[rows, 0:OFF1], in_=o0[:])
+            planes = work.tile([P, D1 * M01], F32, name="pl", tag="pl")
+            for i in range(D1):
+                nc.scalar.activation(out=planes[:, i * M01:(i + 1) * M01], in_=accs[1 + i][:], func=COPY, scale=S01)
+            gt2b = gt2[:].bitcast(BF16).rearrange("p (s n e) -> p s e n", s=D2, n=P, e=2)
+            o2 = outs.tile([P, M2 * D2], F32, name="o2", tag="o2")
+            for (u0, nu) in CHUNKS:
+                pc = bank("pc")
+                pcv = pc[:, 0:D2 * nu].rearrange("p (u i) -> p i u", i=D2)
+                for i in range(D2):
+                    for e in range(2):
+                        c = D2 * e + i
+                        nc.tensor.matmul(
+                            out=pcv[:, i, :],
+                            lhsT=gt2b[:, c // 2, c % 2, :],
+                            rhs=w2t[:, e * M2 + u0:e * M2 + u0 + nu],
+                            start=(e == 0), stop=(e == 1),
+                        )
+                nc.scalar.activation(out=o2[:, D2 * u0:D2 * (u0 + nu)], in_=pc[:, 0:D2 * nu], func=COPY, scale=S2)
+            if k + 1 < NT:
+                q_next = quantise_g(grouped)
+            o1 = outs.tile([P, M01 * D1], F32, name="o1", tag="o1")
+            nc.vector.tensor_copy(
+                out=o1[:].rearrange("p (u i) -> p u i", i=D1),
+                in_=planes[:].rearrange("p (i u) -> p u i", i=D1),
+            )
+            nc.sync.dma_start(out=out[rows, OFF1:OFF2], in_=o1[:])
+            nc.sync.dma_start(out=out[rows, OFF2:COLS], in_=o2[:])

@@ -31,7 +31,7 @@ CHUNKS = ((0, 102), (102, 102), (204, 52))
 FLOPS = 2 * TOKENS * (M01 * M01 * (1 + D1) + M2 * M2 * D2)
 BYTES = 2 * (TOKENS * COLS + 2 * M01 * M01 + M2 * M2) + 4 * TOKENS * COLS
 
-MANUAL = False
+MANUAL = True
 
 
 def tile_linear_kernel(tc, x, w0, w1, w2, grad_out, out):

@@ -118,9 +118,15 @@ def tile_linear_kernel(tc, x, w0, w1, w2, grad_out, out):
             return ta, tb
 
         def evac_block2(tabs):
-            gt2 = work.tile([P, D2 * P], F32, name="gt2", tag="gt2")
-            nc.vector.tensor_copy(out=gt2[:, 0:512], in_=tabs[0][:])
-            nc.vector.tensor_copy(out=gt2[:, 512:640], in_=tabs[1][:, 0:P])
+            gt2 = work.tile([P, 2 * D2 * P], BF16, name="gt2", tag="gt2")
+            nc.vector.tensor_copy(
+                out=gt2[:, 0:8 * P].rearrange("p (s e n) -> p s e n", s=4, e=2, n=P),
+                in_=tabs[0][:].bitcast(BF16).rearrange("p (s n e) -> p s e n", s=4, n=P, e=2),
+            )
+            nc.scalar.copy(
+                out=gt2[:, 8 * P:10 * P].rearrange("p (e n) -> p e n", e=2, n=P),
+                in_=tabs[1][:, 0:P].bitcast(BF16).rearrange("p (n e) -> p e n", n=P, e=2),
+            )
             return gt2
 
         def t_block01(k, srt):
@@ -191,7 +197,6 @@ def tile_linear_kernel(tc, x, w0, w1, w2, grad_out, out):
             planes = work.tile([P, D1 * M01], F32, name="pl", tag="pl")
             for i in range(D1):
                 nc.scalar.activation(out=planes[:, i * M01:(i + 1) * M01], in_=accs[1 + i][:], func=COPY, scale=S01)
-            gt2b = gt2[:].bitcast(BF16).rearrange("p (s n e) -> p s e n", s=D2, n=P, e=2)
             o2 = outs.tile([P, M2 * D2], F32, name="o2", tag="o2")
             for (u0, nu) in CHUNKS:
                 pc = bank("pc")
@@ -201,7 +206,7 @@ def tile_linear_kernel(tc, x, w0, w1, w2, grad_out, out):
                         c = D2 * e + i
                         nc.tensor.matmul(
                             out=pcv[:, i, :],
-                            lhsT=gt2b[:, c // 2, c % 2, :],
+                            lhsT=gt2[:, c * P:(c + 1) * P],
                             rhs=w2t[:, e * M2 + u0:e * M2 + u0 + nu],
                             start=(e == 0), stop=(e == 1),
                         )

@@ -200,17 +200,21 @@ def tile_linear_kernel(tc, x, w0, w1, w2, grad_out, out):
             o2 = outs.tile([P, M2 * D2], F32, name="o2", tag="o2")
             for (u0, nu) in CHUNKS:
                 pc = bank("pc")
-                pcv = pc[:, 0:D2 * nu].rearrange("p (u i) -> p i u", i=D2)
+                pcv = pc[:, 0:D2 * nu].rearrange("p (a i b) -> p i a b", i=D2, b=2)
                 for i in range(D2):
                     for e in range(2):
                         c = D2 * e + i
                         nc.tensor.matmul(
-                            out=pcv[:, i, :],
+                            out=pcv[:, i, :, :],
                             lhsT=gt2[:, c * P:(c + 1) * P],
-                            rhs=w2t[:, e * M2 + u0:e * M2 + u0 + nu],
+                            rhs=w2t[:, e * M2 + u0:e * M2 + u0 + nu].rearrange("p (a b) -> p a b", b=2),
                             start=(e == 0), stop=(e == 1),
                         )
-                nc.scalar.activation(out=o2[:, D2 * u0:D2 * (u0 + nu)], in_=pc[:, 0:D2 * nu], func=COPY, scale=S2)
+                nc.scalar.activation(
+                    out=o2[:, D2 * u0:D2 * (u0 + nu)].rearrange("p (a b i) -> p a b i", b=2, i=D2),
+                    in_=pc[:, 0:D2 * nu].rearrange("p (a i b) -> p a b i", i=D2, b=2),
+                    func=COPY, scale=S2,
+                )
             if k + 1 < NT:
                 q_next = quantise_g(grouped)
             o1 = outs.tile([P, M01 * D1], F32, name="o1", tag="o1")

@@ -200,19 +200,18 @@ def tile_linear_kernel(tc, x, w0, w1, w2, grad_out, out):
             o2 = outs.tile([P, M2 * D2], F32, name="o2", tag="o2")
             for (u0, nu) in CHUNKS:
                 pc = bank("pc")
-                pcv = pc[:, 0:D2 * nu].rearrange("p (a i b) -> p i a b", i=D2, b=2)
                 for i in range(D2):
                     for e in range(2):
                         c = D2 * e + i
                         nc.tensor.matmul(
-                            out=pcv[:, i, :, :],
+                            out=pc[:, i * nu:(i + 1) * nu],
                             lhsT=gt2[:, c * P:(c + 1) * P],
-                            rhs=w2t[:, e * M2 + u0:e * M2 + u0 + nu].rearrange("p (a b) -> p a b", b=2),
+                            rhs=w2t[:, e * M2 + u0:e * M2 + u0 + nu],
                             start=(e == 0), stop=(e == 1),
                         )
                 nc.scalar.activation(
-                    out=o2[:, D2 * u0:D2 * (u0 + nu)].rearrange("p (a b i) -> p a b i", b=2, i=D2),
-                    in_=pc[:, 0:D2 * nu].rearrange("p (a i b) -> p a b i", i=D2, b=2),
+                    out=o2[:, D2 * u0:D2 * (u0 + nu)].rearrange("p (u i) -> p u i", i=D2),
+                    in_=pc[:, 0:D2 * nu].rearrange("p (i u) -> p u i", i=D2),
                     func=COPY, scale=S2,
                 )
             if k + 1 < NT:

@@ -119,14 +119,9 @@ def tile_linear_kernel(tc, x, w0, w1, w2, grad_out, out):
 
         def evac_block2(tabs):
             gt2 = work.tile([P, 2 * D2 * P], BF16, name="gt2", tag="gt2")
-            nc.vector.tensor_copy(
-                out=gt2[:, 0:8 * P].rearrange("p (s e n) -> p s e n", s=4, e=2, n=P),
-                in_=tabs[0][:].bitcast(BF16).rearrange("p (s n e) -> p s e n", s=4, n=P, e=2),
-            )
-            nc.scalar.copy(
-                out=gt2[:, 8 * P:10 * P].rearrange("p (e n) -> p e n", e=2, n=P),
-                in_=tabs[1][:, 0:P].bitcast(BF16).rearrange("p (n e) -> p e n", n=P, e=2),
-            )
+            w32 = gt2[:].bitcast(F32)
+            nc.vector.tensor_copy(out=w32[:, 0:4 * P], in_=tabs[0][:])
+            nc.scalar.copy(out=w32[:, 4 * P:5 * P], in_=tabs[1][:, 0:P])
             return gt2
 
         def t_block01(k, srt):
@@ -192,7 +187,7 @@ def tile_linear_kernel(tc, x, w0, w1, w2, grad_out, out):
                 regroup(ta_next, grouped, ("v", "v"))
                 gt2_next = evac_block2(tb_next)
             o0 = outs.tile([P, M01], F32, name="o0", tag="o0")
-            nc.scalar.activation(out=o0[:], in_=accs[0][:], func=COPY, scale=S01)
+            nc.vector.tensor_scalar(out=o0[:], in0=accs[0][:], scalar1=S01, scalar2=None, op0=MULT)
             nc.sync.dma_start(out=out[rows, 0:OFF1], in_=o0[:])
             planes = work.tile([P, D1 * M01], F32, name="pl", tag="pl")
             for i in range(D1):
@@ -205,7 +200,7 @@ def tile_linear_kernel(tc, x, w0, w1, w2, grad_out, out):
                         c = D2 * e + i
                         nc.tensor.matmul(
                             out=pc[:, i * nu:(i + 1) * nu],
-                            lhsT=gt2[:, c * P:(c + 1) * P],
+                            lhsT=gt2[:, (c // 2) * 2 * P + c % 2:(c // 2 + 1) * 2 * P:2],
                             rhs=w2t[:, e * M2 + u0:e * M2 + u0 + nu],
                             start=(e == 0), stop=(e == 1),
                         )

@@ -53,14 +53,8 @@ def tile_linear_kernel(tc, x, w0, w1, w2, grad_out, out):
 
         load_g(0)
         for b, w in enumerate((w0, w1)):
-            nc.sync.dma_start(
-                out=w_raw[b][:].rearrange("p (a w) -> p a w", a=4),
-                in_=w.rearrange("(a p) w -> p a w", p=P),
-            )
-        nc.sync.dma_start(
-            out=w2_raw[:].rearrange("p (a w) -> p a w", a=2),
-            in_=w2.rearrange("(a p) w -> p a w", p=P),
-        )
+            nc.sync.dma_start(out=w_raw[b][:], in_=w.rearrange("(p a) w -> p (a w)", p=P))
+        nc.sync.dma_start(out=w2_raw[:], in_=w2.rearrange("(p a) w -> p (a w)", p=P))
         for k in range(1, NT):
             load_g(k)
 
@@ -93,11 +87,18 @@ def tile_linear_kernel(tc, x, w0, w1, w2, grad_out, out):
                 banks.append(t)
             return banks
 
-        def regroup(banks, grouped, engines):
-            g32 = grouped[:].bitcast(F32).rearrange("p (r n h) -> p r n h", r=4, n=P, h=2)
+        def regroup(banks, grouped, engines, rows_inner=False):
+            if rows_inner:
+                g32 = grouped[:].bitcast(F32).rearrange("p (n r h) -> p n r h", r=4, n=P, h=2)
+            else:
+                g32 = grouped[:].bitcast(F32).rearrange("p (r n h) -> p r n h", r=4, n=P, h=2)
             for b in range(2):
-                src = banks[b][:].rearrange("p (r h n) -> p r n h", r=2, h=2, n=P)
-                dst = g32[:, 2 * b:2 * b + 2, :, :]
+                if rows_inner:
+                    src = banks[b][:].rearrange("p (r h n) -> p n r h", r=2, h=2, n=P)
+                    dst = g32[:, :, 2 * b:2 * b + 2, :]
+                else:
+                    src = banks[b][:].rearrange("p (r h n) -> p r n h", r=2, h=2, n=P)
+                    dst = g32[:, 2 * b:2 * b + 2, :, :]
                 if engines[b] == "v":
                     nc.vector.tensor_copy(out=dst, in_=src)
                 else:
@@ -144,7 +145,7 @@ def tile_linear_kernel(tc, x, w0, w1, w2, grad_out, out):
             wbanks.append(word_transposes([w32[:, 256 * a:256 * (a + 1)] for a in range(4)]))
         gt2_next = evac_block2(tb_next)
         for b in range(2):
-            regroup(wbanks[b], w_grouped[b], ("s", "v"))
+            regroup(wbanks[b], w_grouped[b], ("s", "v"), rows_inner=True)
         tw2 = bank("tw2")
         w232 = w2_raw[:].bitcast(F32)
         for a in range(2):
@@ -153,8 +154,8 @@ def tile_linear_kernel(tc, x, w0, w1, w2, grad_out, out):
         for b in range(2):
             nc.vector.quantize_mx(out=w_codes[b][:].bitcast(E4X4), scales=w_scales[b][:], in_=w_grouped[b][:])
         nc.scalar.copy(
-            out=w2t[:].rearrange("p (e a u) -> p e a u", e=2, a=2, u=P),
-            in_=tw2[:, 0:2 * P].bitcast(BF16).rearrange("p (a u e) -> p e a u", a=2, u=P, e=2),
+            out=w2t[:].rearrange("p (e u a) -> p e u a", e=2, a=2, u=P),
+            in_=tw2[:, 0:2 * P].bitcast(BF16).rearrange("p (a u e) -> p e u a", a=2, u=P, e=2),
         )
         grouped = work.tile([P, 16 * P], BF16, name="grp", tag="grp", align_bytes=64)
         regroup(ta_next, grouped, ("s", "v"))
@@ -186,13 +187,17 @@ def tile_linear_kernel(tc, x, w0, w1, w2, grad_out, out):
                 grouped = work.tile([P, 16 * P], BF16, name="grp", tag="grp", align_bytes=64)
                 regroup(ta_next, grouped, ("v", "v"))
                 gt2_next = evac_block2(tb_next)
-            o0 = outs.tile([P, M01], F32, name="o0", tag="o0")
-            nc.vector.tensor_scalar(out=o0[:], in0=accs[0][:], scalar1=S01, scalar2=None, op0=MULT)
-            nc.sync.dma_start(out=out[rows, 0:OFF1], in_=o0[:])
+            o_all = outs.tile([P, COLS], F32, name="oall", tag="oall")
+            o0 = o_all[:, 0:OFF1]
+            o1 = o_all[:, OFF1:OFF2]
+            o2 = o_all[:, OFF2:COLS]
+            last = k == NT - 1
+            nc.vector.tensor_scalar(out=o0, in0=accs[0][:], scalar1=S01, scalar2=None, op0=MULT)
+            if last:
+                nc.sync.dma_start(out=out[rows, 0:OFF1], in_=o0)
             planes = work.tile([P, D1 * M01], F32, name="pl", tag="pl")
             for i in range(D1):
                 nc.scalar.activation(out=planes[:, i * M01:(i + 1) * M01], in_=accs[1 + i][:], func=COPY, scale=S01)
-            o2 = outs.tile([P, M2 * D2], F32, name="o2", tag="o2")
             for (u0, nu) in CHUNKS:
                 pc = bank("pc")
                 for i in range(D2):
@@ -211,10 +216,12 @@ def tile_linear_kernel(tc, x, w0, w1, w2, grad_out, out):
                 )
             if k + 1 < NT:
                 q_next = quantise_g(grouped)
-            o1 = outs.tile([P, M01 * D1], F32, name="o1", tag="o1")
             nc.vector.tensor_copy(
-                out=o1[:].rearrange("p (u i) -> p u i", i=D1),
+                out=o1.rearrange("p (u i) -> p u i", i=D1),
                 in_=planes[:].rearrange("p (i u) -> p u i", i=D1),
             )
-            nc.sync.dma_start(out=out[rows, OFF1:OFF2], in_=o1[:])
-            nc.sync.dma_start(out=out[rows, OFF2:COLS], in_=o2[:])
+            if last:
+                nc.sync.dma_start(out=out[rows, OFF2:COLS], in_=o2)
+                nc.sync.dma_start(out=out[rows, OFF1:OFF2], in_=o1)
+            else:
+                nc.sync.dma_start(out=out[rows, :], in_=o_all[:])

@@ -161,15 +161,7 @@ def tile_linear_kernel(tc, x, w0, w1, w2, grad_out, out):
         regroup(ta_next, grouped, ("s", "v"))
         q_next = quantise_g(grouped)
 
-        for k in range(NT):
-            codes, scales = q_next
-            gt2 = gt2_next
-            rows = slice(k * P, (k + 1) * P)
-            if k + 2 < NT:
-                srts[k + 2] = presort(k + 2)
-            if k + 1 < NT:
-                ta_next = t_block01(k + 1, srts[k + 1])
-                tb_next = t_block2(k + 1)
+        def mx_passes(codes, scales):
             accs = []
             for r in range(4):
                 acc = bank("acc")
@@ -183,21 +175,9 @@ def tile_linear_kernel(tc, x, w0, w1, w2, grad_out, out):
                     start=True, stop=True,
                 )
                 accs.append(acc)
-            if k + 1 < NT:
-                grouped = work.tile([P, 16 * P], BF16, name="grp", tag="grp", align_bytes=64)
-                regroup(ta_next, grouped, ("v", "v"))
-                gt2_next = evac_block2(tb_next)
-            o_all = outs.tile([P, COLS], F32, name="oall", tag="oall")
-            o0 = o_all[:, 0:OFF1]
-            o1 = o_all[:, OFF1:OFF2]
-            o2 = o_all[:, OFF2:COLS]
-            last = k == NT - 1
-            nc.vector.tensor_scalar(out=o0, in0=accs[0][:], scalar1=S01, scalar2=None, op0=MULT)
-            if last:
-                nc.sync.dma_start(out=out[rows, 0:OFF1], in_=o0)
-            planes = work.tile([P, D1 * M01], F32, name="pl", tag="pl")
-            for i in range(D1):
-                nc.scalar.activation(out=planes[:, i * M01:(i + 1) * M01], in_=accs[1 + i][:], func=COPY, scale=S01)
+            return accs
+
+        def block2(gt2, o2):
             for (u0, nu) in CHUNKS:
                 pc = bank("pc")
                 for i in range(D2):
@@ -214,7 +194,49 @@ def tile_linear_kernel(tc, x, w0, w1, w2, grad_out, out):
                     in_=pc[:, 0:D2 * nu].rearrange("p (i u) -> p u i", i=D2),
                     func=COPY, scale=S2,
                 )
-            if k + 1 < NT:
+
+        def blocks01_out(accs, o0, planes):
+            nc.vector.tensor_scalar(out=o0, in0=accs[0][:], scalar1=S01, scalar2=None, op0=MULT)
+            for i in range(D1):
+                nc.scalar.activation(out=planes[:, i * M01:(i + 1) * M01], in_=accs[1 + i][:], func=COPY, scale=S01)
+
+        def turn(k1):
+            return t_block01(k1, srts[k1]), t_block2(k1)
+
+        def turned_out(banks01, banks2):
+            grouped = work.tile([P, 16 * P], BF16, name="grp", tag="grp", align_bytes=64)
+            regroup(banks01, grouped, ("v", "v"))
+            return grouped, evac_block2(banks2)
+
+        for k in range(NT):
+            codes, scales = q_next
+            gt2 = gt2_next
+            rows = slice(k * P, (k + 1) * P)
+            last = k == NT - 1
+            o_all = outs.tile([P, COLS], F32, name="oall", tag="oall")
+            o0 = o_all[:, 0:OFF1]
+            o1 = o_all[:, OFF1:OFF2]
+            o2 = o_all[:, OFF2:COLS]
+            planes = work.tile([P, D1 * M01], F32, name="pl", tag="pl")
+            if k + 2 < NT:
+                srts[k + 2] = presort(k + 2)
+            if k == 0:
+                block2(gt2, o2)
+                accs = mx_passes(codes, scales)
+                blocks01_out(accs, o0, planes)
+                banks01, banks2 = turn(1)
+                grouped, gt2_next = turned_out(banks01, banks2)
+            else:
+                if not last:
+                    banks01, banks2 = turn(k + 1)
+                accs = mx_passes(codes, scales)
+                if not last:
+                    grouped, gt2_next = turned_out(banks01, banks2)
+                blocks01_out(accs, o0, planes)
+                if last:
+                    nc.sync.dma_start(out=out[rows, 0:OFF1], in_=o0)
+                block2(gt2, o2)
+            if not last:
                 q_next = quantise_g(grouped)
             nc.vector.tensor_copy(
                 out=o1.rearrange("p (u i) -> p u i", i=D1),

@@ -39,7 +39,7 @@ def tile_linear_kernel(tc, x, w0, w1, w2, grad_out, out):
     with ExitStack() as ctx:
         keep = ctx.enter_context(tc.tile_pool(name="keep", bufs=1))
         work = ctx.enter_context(tc.tile_pool(name="work", bufs=2))
-        outs = ctx.enter_context(tc.tile_pool(name="outs", bufs=3))
+        outs = ctx.enter_context(tc.tile_pool(name="outs", bufs=6))
         psum = ctx.enter_context(tc.psum_pool(name="psum", bufs=8))
         if MANUAL:
             ctx.enter_context(tc.manual_schedule())
@@ -65,7 +65,7 @@ def tile_linear_kernel(tc, x, w0, w1, w2, grad_out, out):
             return psum.tile([P, 512], F32, name=name, tag="bank")
 
         def presort(k):
-            srt = work.tile([P, M01 * D1], BF16, name="srt", tag="srt", bufs=3)
+            srt = work.tile([P, M01 * D1], BF16, name="srt", tag="srt", bufs=1)
             nc.gpsimd.tensor_scalar(
                 out=srt[:].rearrange("p (i w) -> p i w", i=D1),
                 in0=g_sb[k][:, OFF1:OFF2].rearrange("p (w i) -> p i w", i=D1),
@@ -137,7 +137,7 @@ def tile_linear_kernel(tc, x, w0, w1, w2, grad_out, out):
             nc.vector.quantize_mx(out=codes[:].bitcast(E5X4), scales=scales[:], in_=grouped[:])
             return codes, scales
 
-        srts = {0: presort(0), 1: presort(1)}
+        srts = {0: presort(0)}
         tb_next = t_block2(0)
         wbanks = []
         for b in range(2):
@@ -151,6 +151,7 @@ def tile_linear_kernel(tc, x, w0, w1, w2, grad_out, out):
         for a in range(2):
             nc.tensor.transpose(out=tw2[:, a * P:(a + 1) * P], in_=w232[:, a * P:(a + 1) * P], identity=ident[:])
         ta_next = t_block01(0, srts[0])
+        srts[1] = presort(1)
         for b in range(2):
             nc.vector.quantize_mx(out=w_codes[b][:].bitcast(E4X4), scales=w_scales[b][:], in_=w_grouped[b][:])
         nc.scalar.copy(
@@ -217,24 +218,20 @@ def tile_linear_kernel(tc, x, w0, w1, w2, grad_out, out):
             o0 = o_all[:, 0:OFF1]
             o1 = o_all[:, OFF1:OFF2]
             o2 = o_all[:, OFF2:COLS]
-            planes = work.tile([P, D1 * M01], F32, name="pl", tag="pl")
-            if k + 2 < NT:
-                srts[k + 2] = presort(k + 2)
+            planes = work.tile([P, D1 * M01], F32, name="pl", tag="pl", bufs=3)
             if k == 0:
                 block2(gt2, o2)
-                accs = mx_passes(codes, scales)
-                blocks01_out(accs, o0, planes)
-                banks01, banks2 = turn(1)
+            if not last:
+                banks01, banks2 = turn(k + 1)
+            if k + 2 < NT:
+                srts[k + 2] = presort(k + 2)
+            accs = mx_passes(codes, scales)
+            if not last:
                 grouped, gt2_next = turned_out(banks01, banks2)
-            else:
-                if not last:
-                    banks01, banks2 = turn(k + 1)
-                accs = mx_passes(codes, scales)
-                if not last:
-                    grouped, gt2_next = turned_out(banks01, banks2)
-                blocks01_out(accs, o0, planes)
-                if last:
-                    nc.sync.dma_start(out=out[rows, 0:OFF1], in_=o0)
+            blocks01_out(accs, o0, planes)
+            if last:
+                nc.sync.dma_start(out=out[rows, 0:OFF1], in_=o0)
+            if k > 0:
                 block2(gt2, o2)
             if not last:
                 q_next = quantise_g(grouped)

@@ -32,6 +32,7 @@ FLOPS = 2 * TOKENS * (M01 * M01 * (1 + D1) + M2 * M2 * D2)
 BYTES = 2 * (TOKENS * COLS + 2 * M01 * M01 + M2 * M2) + 4 * TOKENS * COLS
 
 MANUAL = True
+O2_CUT = 1016
 
 
 def tile_linear_kernel(tc, x, w0, w1, w2, grad_out, out):
@@ -196,10 +197,20 @@ def tile_linear_kernel(tc, x, w0, w1, w2, grad_out, out):
                     func=COPY, scale=S2,
                 )
 
-        def blocks01_out(accs, o0, planes):
+        def blocks01_out(accs, o0, planes, shared):
             nc.vector.tensor_scalar(out=o0, in0=accs[0][:], scalar1=S01, scalar2=None, op0=MULT)
             for i in range(D1):
-                nc.scalar.activation(out=planes[:, i * M01:(i + 1) * M01], in_=accs[1 + i][:], func=COPY, scale=S01)
+                plane = planes[:, i * M01:(i + 1) * M01]
+                if shared and i == D1 - 1:
+                    nc.vector.tensor_scalar(out=plane, in0=accs[1 + i][:], scalar1=S01, scalar2=None, op0=MULT)
+                else:
+                    nc.scalar.activation(out=plane, in_=accs[1 + i][:], func=COPY, scale=S01)
+
+        def interleave(o1, planes, u0, u1):
+            nc.vector.tensor_copy(
+                out=o1[:, D1 * u0:D1 * u1].rearrange("p (u i) -> p u i", i=D1),
+                in_=planes[:].rearrange("p (i u) -> p u i", i=D1)[:, u0:u1, :],
+            )
 
         def turn(k1):
             return t_block01(k1, srts[k1]), t_block2(k1)
@@ -228,19 +239,20 @@ def tile_linear_kernel(tc, x, w0, w1, w2, grad_out, out):
             accs = mx_passes(codes, scales)
             if not last:
                 grouped, gt2_next = turned_out(banks01, banks2)
-            blocks01_out(accs, o0, planes)
+            blocks01_out(accs, o0, planes, last)
             if last:
                 nc.sync.dma_start(out=out[rows, 0:OFF1], in_=o0)
             if k > 0:
                 block2(gt2, o2)
             if not last:
                 q_next = quantise_g(grouped)
-            nc.vector.tensor_copy(
-                out=o1.rearrange("p (u i) -> p u i", i=D1),
-                in_=planes[:].rearrange("p (i u) -> p u i", i=D1),
-            )
             if last:
-                nc.sync.dma_start(out=out[rows, OFF2:COLS], in_=o2)
-                nc.sync.dma_start(out=out[rows, OFF1:OFF2], in_=o1)
+                for u0 in range(0, M01, M01 // 2):
+                    interleave(o1, planes, u0, u0 + M01 // 2)
+                    cols = slice(OFF1 + D1 * u0, OFF1 + D1 * (u0 + M01 // 2))
+                    nc.sync.dma_start(out=out[rows, cols], in_=o_all[:, cols])
+                nc.sync.dma_start(out=out[rows, OFF2:OFF2 + O2_CUT], in_=o_all[:, OFF2:OFF2 + O2_CUT])
+                nc.sync.dma_start(out=out[rows, OFF2 + O2_CUT:COLS], in_=o_all[:, OFF2 + O2_CUT:COLS])
             else:
+                interleave(o1, planes, 0, M01)
                 nc.sync.dma_start(out=out[rows, :], in_=o_all[:])

import math
from contextlib import ExitStack

import concourse.mybir as mybir
from concourse.masks import make_identity

F32 = mybir.dt.float32
BF16 = mybir.dt.bfloat16
U32 = mybir.dt.uint32
U8 = mybir.dt.uint8
E4X4 = mybir.dt.float8_e4m3fn_x4
E5X4 = mybir.dt.float8_e5m2_x4
COPY = mybir.ActivationFunctionType.Copy
MULT = mybir.AluOpType.mult
ADD = mybir.AluOpType.add

P = 128
TOKENS = 1024
NT = TOKENS // P
M01 = 512
M2 = 256
D1 = 3
D2 = 5
OFF1 = M01
OFF2 = M01 + M01 * D1
COLS = OFF2 + M2 * D2
S01 = 1.0 / math.sqrt(M01)
S2 = 1.0 / math.sqrt(M2)
CHUNKS = ((0, 102), (102, 102), (204, 52))

FLOPS = 2 * TOKENS * (M01 * M01 * (1 + D1) + M2 * M2 * D2)
BYTES = 2 * (TOKENS * COLS + 2 * M01 * M01 + M2 * M2) + 4 * TOKENS * COLS

MANUAL = True
O2_CUT = 1016


def tile_linear_kernel(tc, x, w0, w1, w2, grad_out, out):
    nc = tc.nc
    with ExitStack() as ctx:
        keep = ctx.enter_context(tc.tile_pool(name="keep", bufs=1))
        work = ctx.enter_context(tc.tile_pool(name="work", bufs=2))
        outs = ctx.enter_context(tc.tile_pool(name="outs", bufs=6))
        psum = ctx.enter_context(tc.psum_pool(name="psum", bufs=8))
        if MANUAL:
            ctx.enter_context(tc.manual_schedule())

        g_sb = [keep.tile([P, COLS], BF16, name="g%d" % k) for k in range(NT)]
        w_raw = [keep.tile([P, 4 * M01], BF16, name="wraw%d" % b) for b in range(2)]
        w2_raw = keep.tile([P, 2 * M2], BF16, name="w2raw")

        def load_g(k):
            nc.sync.dma_start(out=g_sb[k][:], in_=grad_out[k * P:(k + 1) * P, :])

        load_g(0)
        for b, w in enumerate((w0, w1)):
            nc.sync.dma_start(out=w_raw[b][:], in_=w.rearrange("(p a) w -> p (a w)", p=P))
        nc.sync.dma_start(out=w2_raw[:], in_=w2.rearrange("(p a) w -> p (a w)", p=P))
        for k in range(1, NT):
            load_g(k)

        ident = keep.tile([P, P], F32, name="ident")
        make_identity(nc, ident[:])

        def bank(name):
            return psum.tile([P, 512], F32, name=name, tag="bank")

        def presort(k):
            srt = work.tile([P, M01 * D1], BF16, name="srt", tag="srt", bufs=1)
            nc.gpsimd.tensor_scalar(
                out=srt[:].rearrange("p (i w) -> p i w", i=D1),
                in0=g_sb[k][:, OFF1:OFF2].rearrange("p (w i) -> p i w", i=D1),
                scalar1=1.0, scalar2=0.0, op0=MULT, op1=ADD,
            )
            return srt

        def word_transposes(rows):
            banks = []
            for b in range(2):
                t = bank("tw")
                for r in range(2):
                    for h in range(2):
                        nc.tensor.transpose(
                            out=t[:, (2 * r + h) * P:(2 * r + h + 1) * P],
                            in_=rows[2 * b + r][:, h * P:(h + 1) * P],
                            identity=ident[:],
                        )
                banks.append(t)
            return banks

        def regroup(banks, grouped, engines, rows_inner=False):
            if rows_inner:
                g32 = grouped[:].bitcast(F32).rearrange("p (n r h) -> p n r h", r=4, n=P, h=2)
            else:
                g32 = grouped[:].bitcast(F32).rearrange("p (r n h) -> p r n h", r=4, n=P, h=2)
            for b in range(2):
                if rows_inner:
                    src = banks[b][:].rearrange("p (r h n) -> p n r h", r=2, h=2, n=P)
                    dst = g32[:, :, 2 * b:2 * b + 2, :]
                else:
                    src = banks[b][:].rearrange("p (r h n) -> p r n h", r=2, h=2, n=P)
                    dst = g32[:, 2 * b:2 * b + 2, :, :]
                if engines[b] == "v":
                    nc.vector.tensor_copy(out=dst, in_=src)
                else:
                    nc.scalar.copy(out=dst, in_=src)

        w_codes = [keep.tile([P, M01], U32, name="wc%d" % b, align_bytes=64) for b in range(2)]
        w_scales = [keep.tile([P, M01], U8, name="ws%d" % b, align_bytes=64) for b in range(2)]
        w_grouped = [keep.tile([P, 4 * M01], BF16, name="wg%d" % b, align_bytes=64) for b in range(2)]
        w2t = keep.tile([P, 2 * M2], BF16, name="w2t")

        def t_block2(k):
            g32 = g_sb[k][:].bitcast(F32)[:, OFF2 // 2:COLS // 2].rearrange("p (j s) -> p s j", s=D2)
            ta = bank("tb")
            for s in range(4):
                nc.tensor.transpose(out=ta[:, s * P:(s + 1) * P], in_=g32[:, s, :], identity=ident[:])
            tb = bank("tb")
            nc.tensor.transpose(out=tb[:, 0:P], in_=g32[:, 4, :], identity=ident[:])
            return ta, tb

        def evac_block2(tabs):
            gt2 = work.tile([P, 2 * D2 * P], BF16, name="gt2", tag="gt2")
            w32 = gt2[:].bitcast(F32)
            nc.vector.tensor_copy(out=w32[:, 0:4 * P], in_=tabs[0][:])
            nc.scalar.copy(out=w32[:, 4 * P:5 * P], in_=tabs[1][:, 0:P])
            return gt2

        def t_block01(k, srt):
            g32 = g_sb[k][:].bitcast(F32)
            s32 = srt[:].bitcast(F32)
            rows = [g32[:, 0:256]] + [s32[:, 256 * i:256 * (i + 1)] for i in range(D1)]
            return word_transposes(rows)

        def quantise_g(grouped):
            codes = work.tile([P, 4 * P], U32, name="gc", tag="gc", align_bytes=64)
            scales = work.tile([P, 4 * P], U8, name="gs", tag="gs", align_bytes=64)
            nc.vector.quantize_mx(out=codes[:].bitcast(E5X4), scales=scales[:], in_=grouped[:])
            return codes, scales

        srts = {0: presort(0)}
        tb_next = t_block2(0)
        wbanks = []
        for b in range(2):
            w32 = w_raw[b][:].bitcast(F32)
            wbanks.append(word_transposes([w32[:, 256 * a:256 * (a + 1)] for a in range(4)]))
        gt2_next = evac_block2(tb_next)
        for b in range(2):
            regroup(wbanks[b], w_grouped[b], ("s", "v"), rows_inner=True)
        tw2 = bank("tw2")
        w232 = w2_raw[:].bitcast(F32)
        for a in range(2):
            nc.tensor.transpose(out=tw2[:, a * P:(a + 1) * P], in_=w232[:, a * P:(a + 1) * P], identity=ident[:])
        ta_next = t_block01(0, srts[0])
        srts[1] = presort(1)
        for b in range(2):
            nc.vector.quantize_mx(out=w_codes[b][:].bitcast(E4X4), scales=w_scales[b][:], in_=w_grouped[b][:])
        nc.scalar.copy(
            out=w2t[:].rearrange("p (e u a) -> p e u a", e=2, a=2, u=P),
            in_=tw2[:, 0:2 * P].bitcast(BF16).rearrange("p (a u e) -> p e u a", a=2, u=P, e=2),
        )
        grouped = work.tile([P, 16 * P], BF16, name="grp", tag="grp", align_bytes=64)
        regroup(ta_next, grouped, ("s", "v"))
        q_next = quantise_g(grouped)

        def mx_passes(codes, scales):
            accs = []
            for r in range(4):
                acc = bank("acc")
                b = min(r, 1)
                nc.tensor.matmul_mx(
                    out=acc[:],
                    lhsT=codes[:, r * P:(r + 1) * P].bitcast(E5X4),
                    lhsT_scale=scales[:, r * P:(r + 1) * P],
                    rhs=w_codes[b][:].bitcast(E4X4),
                    rhs_scale=w_scales[b][:],
                    start=True, stop=True,
                )
                accs.append(acc)
            return accs

        def block2(gt2, o2):
            for (u0, nu) in CHUNKS:
                pc = bank("pc")
                for i in range(D2):
                    for e in range(2):
                        c = D2 * e + i
                        nc.tensor.matmul(
                            out=pc[:, i * nu:(i + 1) * nu],
                            lhsT=gt2[:, (c // 2) * 2 * P + c % 2:(c // 2 + 1) * 2 * P:2],
                            rhs=w2t[:, e * M2 + u0:e * M2 + u0 + nu],
                            start=(e == 0), stop=(e == 1),
                        )
                nc.scalar.activation(
                    out=o2[:, D2 * u0:D2 * (u0 + nu)].rearrange("p (u i) -> p u i", i=D2),
                    in_=pc[:, 0:D2 * nu].rearrange("p (i u) -> p u i", i=D2),
                    func=COPY, scale=S2,
                )

        def blocks01_out(accs, o0, planes, shared):
            nc.vector.tensor_scalar(out=o0, in0=accs[0][:], scalar1=S01, scalar2=None, op0=MULT)
            for i in range(D1):
                plane = planes[:, i * M01:(i + 1) * M01]
                if shared and i == D1 - 1:
                    nc.vector.tensor_scalar(out=plane, in0=accs[1 + i][:], scalar1=S01, scalar2=None, op0=MULT)
                else:
                    nc.scalar.activation(out=plane, in_=accs[1 + i][:], func=COPY, scale=S01)

        def interleave(o1, planes, u0, u1):
            nc.vector.tensor_copy(
                out=o1[:, D1 * u0:D1 * u1].rearrange("p (u i) -> p u i", i=D1),
                in_=planes[:].rearrange("p (i u) -> p u i", i=D1)[:, u0:u1, :],
            )

        def turn(k1):
            return t_block01(k1, srts[k1]), t_block2(k1)

        def turned_out(banks01, banks2):
            grouped = work.tile([P, 16 * P], BF16, name="grp", tag="grp", align_bytes=64)
            regroup(banks01, grouped, ("v", "v"))
            return grouped, evac_block2(banks2)

        for k in range(NT):
            codes, scales = q_next
            gt2 = gt2_next
            rows = slice(k * P, (k + 1) * P)
            last = k == NT - 1
            o_all = outs.tile([P, COLS], F32, name="oall", tag="oall")
            o0 = o_all[:, 0:OFF1]
            o1 = o_all[:, OFF1:OFF2]
            o2 = o_all[:, OFF2:COLS]
            planes = work.tile([P, D1 * M01], F32, name="pl", tag="pl", bufs=3)
            if k == 0:
                block2(gt2, o2)
            if not last:
                banks01, banks2 = turn(k + 1)
            if k + 2 < NT:
                srts[k + 2] = presort(k + 2)
            accs = mx_passes(codes, scales)
            if not last:
                grouped, gt2_next = turned_out(banks01, banks2)
            blocks01_out(accs, o0, planes, last)
            if last:
                nc.sync.dma_start(out=out[rows, 0:OFF1], in_=o0)
            if k > 0:
                block2(gt2, o2)
            if not last:
                q_next = quantise_g(grouped)
            if last:
                for u0 in range(0, M01, M01 // 2):
                    interleave(o1, planes, u0, u0 + M01 // 2)
                    cols = slice(OFF1 + D1 * u0, OFF1 + D1 * (u0 + M01 // 2))
                    nc.sync.dma_start(out=out[rows, cols], in_=o_all[:, cols])
                nc.sync.dma_start(out=out[rows, OFF2:OFF2 + O2_CUT], in_=o_all[:, OFF2:OFF2 + O2_CUT])
                nc.sync.dma_start(out=out[rows, OFF2 + O2_CUT:COLS], in_=o_all[:, OFF2 + O2_CUT:COLS])
            else:
                interleave(o1, planes, 0, M01)
                nc.sync.dma_start(out=out[rows, :], in_=o_all[:])
